import numpy as np
import ml_dtypes


def mxq(x, axis, fmt="e4m3"):
    dtype, down = {"e4m3": (ml_dtypes.float8_e4m3fn, 7), "e5m2": (ml_dtypes.float8_e5m2, 14)}[fmt]
    v = np.moveaxis(np.asarray(x, np.float32).astype(ml_dtypes.bfloat16).astype(np.float64), axis, -1)
    blocks = v.reshape(v.shape[:-1] + (-1, 32))
    amax = np.abs(blocks).max(-1, keepdims=True)
    byte = np.maximum(np.where(amax > 0, np.frexp(amax)[1] - 1 + 127, 0) - down, 1)
    scale = np.exp2(byte - 127.0)
    codes = (blocks / scale).astype(np.float32).astype(dtype).astype(np.float64)
    return np.moveaxis((codes * scale).reshape(v.shape), -1, axis)


WIDE = False


def mx_kscale(k):
    if not WIDE:
        return np.ones(k)
    levels = np.array([10, -10, 5, -5, 0])
    a = np.random.permutation(np.resize(levels, k // 512 * 4)).reshape(k // 512, 4)
    idx = np.arange(k)
    return np.exp2(a[idx // 512, idx % 128 // 32])


BF16 = ml_dtypes.bfloat16


def bf(x):
    return np.asarray(x, np.float32).astype(BF16)


def f64(x):
    return np.asarray(x).astype(np.float64)


E2M1 = np.array([0.0, 0.5, 1.0, 1.5, 2.0, 3.0, 4.0, 6.0, -0.0, -0.5, -1.0, -1.5, -2.0, -3.0, -4.0, -6.0])


def pack_weight(w, fmt):
    k, n = w.shape
    w = f64(bf(w)).reshape(k // 32, 32, n)
    amax = np.abs(w).max(1)
    if fmt == "e4m3":
        byte = np.frexp(amax)[1] - 1 + 127 - 7
    else:
        mant, ex = np.frexp(amax / 6.0)
        byte = np.where(mant > 0.5, ex, ex - 1) + 127
    byte = np.clip(np.where(amax > 0, byte, 1), 1, 254)
    scaled = (w * np.exp2(127.0 - byte)[:, None, :]).reshape(k, n).astype(np.float32)
    by_word = np.ascontiguousarray(scaled.reshape(k // 512, 128, 4, n).transpose(0, 1, 3, 2))
    if fmt == "e4m3":
        words = by_word.astype(ml_dtypes.float8_e4m3fn).view(np.uint8)
    else:
        c = by_word.astype(ml_dtypes.float4_e2m1fn).view(np.uint8) & 0xF
        words = c[..., 0::2] | (c[..., 1::2] << 4)
    return np.ascontiguousarray(words), np.ascontiguousarray(byte.astype(np.uint8).reshape(k // 512, 16, n))


def unpack_weight(words, scales, fmt):
    g, p, n, _ = words.shape
    if fmt == "e4m3":
        vals = np.ascontiguousarray(words).view(ml_dtypes.float8_e4m3fn).astype(np.float64)
    else:
        nib = np.empty((g, p, n, 4), np.uint8)
        nib[..., 0::2] = words & 0xF
        nib[..., 1::2] = words >> 4
        vals = E2M1[nib]
    vals = vals * np.repeat(np.exp2(scales.astype(np.float64) - 127.0), 8, axis=1)[..., None]
    return vals.transpose(0, 1, 3, 2).reshape(g * 512, n)


B, I, H = 4096, 512, 512
EPS = 1e-5
FMT = "e4m3"


def sigmoid(v):
    return 1.0 / (1.0 + np.exp(-v))


def ln(v, g, b):
    m = v.mean(-1, keepdims=True)
    var = np.square(v - m).mean(-1, keepdims=True)
    return (v - m) / np.sqrt(var + EPS) * g + b


def setup_inputs():
    s, t = mx_kscale(I), mx_kscale(H)
    d = {"x": bf(np.random.standard_normal((B, I)) * s), "h": bf(np.random.standard_normal((B, H)) * t)}
    for g in ("i", "c"):
        words, scales = pack_weight((np.random.standard_normal((H, I)) / np.sqrt(I) / s[None, :]).T, FMT)
        d["W" + g + "_w_words"] = words
        d["W" + g + "_w_scales"] = scales
        d["W" + g + "_b"] = bf(np.random.standard_normal(H) * 0.5)
        words, scales = pack_weight((np.random.standard_normal((H, H)) / np.sqrt(H) / t[None, :]).T, FMT)
        d["U" + g + "_w_words"] = words
        d["U" + g + "_w_scales"] = scales
        d["ln" + g + "_g"] = bf(1.0 + 0.2 * np.random.standard_normal(H))
        d["ln" + g + "_b"] = bf(0.2 * np.random.standard_normal(H))
    return d


def reference(x, h, Wi_w_words, Wi_w_scales, Wi_b, Ui_w_words, Ui_w_scales, lni_g, lni_b, Wc_w_words, Wc_w_scales, Wc_b, Uc_w_words, Uc_w_scales, lnc_g, lnc_b):
    xq = mxq(f64(x), 1, "e4m3")
    hq = mxq(f64(h), 1, "e4m3")
    pre_i = (xq @ unpack_weight(Wi_w_words, Wi_w_scales, FMT)) + f64(Wi_b) + (hq @ unpack_weight(Ui_w_words, Ui_w_scales, FMT))
    pre_c = (xq @ unpack_weight(Wc_w_words, Wc_w_scales, FMT)) + f64(Wc_b) + (hq @ unpack_weight(Uc_w_words, Uc_w_scales, FMT))
    i = sigmoid(ln(pre_i, f64(lni_g), f64(lni_b)))
    c_tilde = np.tanh(ln(pre_c, f64(lnc_g), f64(lnc_b)))
    return i * c_tilde

@@ -1,0 +1,205 @@
+import concourse.mybir as mybir
+from concourse.masks import make_identity
+
+F32 = mybir.dt.float32
+BF16 = mybir.dt.bfloat16
+U8 = mybir.dt.uint8
+U32 = mybir.dt.uint32
+I32 = mybir.dt.int32
+FP8X4 = mybir.dt.float8_e4m3fn_x4
+ALU = mybir.AluOpType
+ACT = mybir.ActivationFunctionType
+
+P = 128
+B = 4096
+K = 512
+H = 512
+EPS = 1e-5
+SUB = 4
+BLOCK = P * SUB
+N_BLOCKS = B // BLOCK
+FLOPS = 2 * B * (2 * K) * (2 * H)
+
+
+def tile_layernormlstmcell_pa_t_kernel(
+    tc,
+    x,
+    h,
+    Wi_w_words,
+    Wi_w_scales,
+    Wi_b,
+    Ui_w_words,
+    Ui_w_scales,
+    lni_g,
+    lni_b,
+    Wc_w_words,
+    Wc_w_scales,
+    Wc_b,
+    Uc_w_words,
+    Uc_w_scales,
+    lnc_g,
+    lnc_b,
+    out,
+):
+    nc = tc.nc
+    weights = [
+        [(Wi_w_words, Wi_w_scales), (Ui_w_words, Ui_w_scales)],
+        [(Wc_w_words, Wc_w_scales), (Uc_w_words, Uc_w_scales)],
+    ]
+    vectors = [(Wi_b, lni_g, lni_b), (Wc_b, lnc_g, lnc_b)]
+    functions = [ACT.Sigmoid, ACT.Tanh]
+
+    with tc.tile_pool(name="const", bufs=1) as const, tc.tile_pool(
+        name="rows", bufs=3
+    ) as rows, tc.tile_pool(name="quant", bufs=4) as quant, tc.tile_pool(
+        name="work", bufs=4
+    ) as work, tc.tile_pool(name="stat", bufs=8) as stat, tc.psum_pool(
+        name="psum_t", bufs=2
+    ) as psum_t, tc.psum_pool(name="psum_mm", bufs=4) as psum_mm:
+        planes = const.tile([P, H], U8, align_bytes=64)
+        nc.vector.memset(planes[:].bitcast(I32), 0)
+        ident = const.tile([P, P], F32)
+        make_identity(nc, ident[:])
+        neg_half = const.tile([P, 2], F32)
+        nc.vector.memset(neg_half[:], -0.5)
+
+        w_words = []
+        for gate in range(2):
+            for operand in range(2):
+                words_in, scales_in = weights[gate][operand]
+                w = 2 * gate + operand
+                for quad in range(4):
+                    first = 32 * quad + 4 * w
+                    nc.sync.dma_start(
+                        out=planes[first : first + 4, :].bitcast(I32),
+                        in_=scales_in[0, 4 * quad : 4 * quad + 4, :].bitcast(I32),
+                    )
+                words = const.tile([P, H], U32, name="words%d" % w, align_bytes=64)
+                nc.sync.dma_start(
+                    out=words[:].bitcast(I32),
+                    in_=words_in[0].rearrange("p n t -> p (n t)").bitcast(I32),
+                )
+                w_words.append(words)
+
+        spread = []
+        for gate in range(2):
+            for v in range(3):
+                vec = const.tile([P, H], BF16, name="vec%d_%d" % (gate, v))
+                nc.sync.dma_start(out=vec[:], in_=vectors[gate][v].partition_broadcast(P))
+                spread.append(vec)
+
+        for block in range(N_BLOCKS):
+            block_rows = slice(block * BLOCK, (block + 1) * BLOCK)
+            x_sb = rows.tile([P, SUB, K], BF16)
+            nc.scalar.dma_start(
+                out=x_sb[:], in_=x[block_rows, :].rearrange("(p s) k -> p s k", s=SUB)
+            )
+            h_sb = rows.tile([P, SUB, K], BF16)
+            nc.scalar.dma_start(
+                out=h_sb[:], in_=h[block_rows, :].rearrange("(p s) k -> p s k", s=SUB)
+            )
+            o_sb = rows.tile([P, SUB, H], F32)
+
+            for s in range(SUB):
+                flipped = psum_t.tile([P, 4, P], F32)
+                for operand, src in enumerate((x_sb, h_sb)):
+                    pairs = src[:, s, :].bitcast(F32)
+                    for u in range(2):
+                        nc.tensor.transpose(
+                            flipped[:, 2 * operand + u, :], pairs[:, u : K // 2 : 2], ident[:]
+                        )
+                grouped = quant.tile([P, 2 * P * 4], BF16, align_bytes=64)
+                nc.scalar.copy(
+                    out=grouped[:].bitcast(F32).rearrange("p (o r u) -> p o r u", o=2, u=2),
+                    in_=flipped[:].rearrange("p (o u) r -> p o r u", u=2),
+                )
+                codes = quant.tile([P, 2 * P], U32, align_bytes=64)
+                scales = quant.tile([P, 2 * P], U8, align_bytes=64)
+                nc.vector.quantize_mx(
+                    out=codes[:].bitcast(FP8X4), scales=scales[:], in_=grouped[:]
+                )
+
+                z_sum = stat.tile([P, 2], F32)
+                neg_mean = stat.tile([P, 2], F32)
+                sq_sum = stat.tile([P, 2], F32)
+                var_eps = stat.tile([P, 2], F32)
+                rstd = stat.tile([P, 2], F32)
+                z_gate = []
+                for gate in range(2):
+                    acc = psum_mm.tile([P, H], F32)
+                    for operand in range(2):
+                        w = 2 * gate + operand
+                        cols = slice(operand * P, (operand + 1) * P)
+                        nc.tensor.matmul_mx(
+                            out=acc[:],
+                            lhsT=codes[:, cols].bitcast(FP8X4),
+                            lhsT_scale=scales[:, cols],
+                            rhs=w_words[w][:].bitcast(FP8X4),
+                            rhs_scale=planes[4 * w : P, :],
+                            start=(operand == 0),
+                            stop=(operand == 1),
+                        )
+                    z = work.tile([P, H], F32, name="z%d" % gate)
+                    nc.vector.scalar_tensor_tensor(
+                        out=z[:],
+                        in0=acc[:],
+                        scalar=1.0,
+                        in1=spread[3 * gate][:],
+                        op0=ALU.mult,
+                        op1=ALU.add,
+                        accum_out=z_sum[:, gate : gate + 1],
+                    )
+                    z_gate.append(z)
+                nc.vector.tensor_scalar(
+                    out=neg_mean[:], in0=z_sum[:], scalar1=-1.0 / H, scalar2=None, op0=ALU.mult
+                )
+                for gate in range(2):
+                    squares = work.tile([P, H], BF16, name="squares%d" % gate)
+                    nc.scalar.activation(
+                        out=squares[:],
+                        in_=z_gate[gate][:],
+                        func=ACT.Square,
+                        bias=neg_mean[:, gate : gate + 1],
+                        scale=1.0,
+                        accum_out=sq_sum[:, gate : gate + 1],
+                    )
+                nc.vector.tensor_scalar(
+                    out=var_eps[:],
+                    in0=sq_sum[:],
+                    scalar1=1.0 / H,
+                    scalar2=EPS,
+                    op0=ALU.mult,
+                    op1=ALU.add,
+                )
+                nc.gpsimd.tensor_tensor(
+                    out=rstd[:], in0=var_eps[:], in1=neg_half[:], op=ALU.pow
+                )
+                acted = []
+                for gate in range(2):
+                    scaled = work.tile([P, H], F32, name="scaled%d" % gate)
+                    nc.vector.scalar_tensor_tensor(
+                        out=scaled[:],
+                        in0=z_gate[gate][:],
+                        scalar=neg_mean[:, gate : gate + 1],
+                        in1=spread[3 * gate + 1][:],
+                        op0=ALU.add,
+                        op1=ALU.mult,
+                    )
+                    shifted = work.tile([P, H], F32, name="shifted%d" % gate)
+                    nc.vector.scalar_tensor_tensor(
+                        out=shifted[:],
+                        in0=scaled[:],
+                        scalar=rstd[:, gate : gate + 1],
+                        in1=spread[3 * gate + 2][:],
+                        op0=ALU.mult,
+                        op1=ALU.add,
+                    )
+                    a = work.tile([P, H], F32, name="acted%d" % gate)
+                    nc.scalar.activation(out=a[:], in_=shifted[:], func=functions[gate])
+                    acted.append(a)
+                nc.vector.tensor_tensor(
+                    out=o_sb[:, s, :], in0=acted[0][:], in1=acted[1][:], op=ALU.mult
+                )
+            nc.sync.dma_start(
+                out=out[block_rows, :].rearrange("(p s) n -> p s n", s=SUB), in_=o_sb[:]
+            )

@@ -14,11 +14,21 @@ P = 128
 B = 4096
 K = 512
 H = 512
+H_TILES = H // P
 EPS = 1e-5
 SUB = 4
 BLOCK = P * SUB
 N_BLOCKS = B // BLOCK
-FLOPS = 2 * B * (2 * K) * (2 * H)
+N_TILES = B // P
+GATES = 2
+FLOPS = 2 * B * (2 * K) * (GATES * H)
+
+FLIP_AHEAD = 2
+QUANT_AHEAD = 1
+NORM_BEHIND = 1
+TURN_BEHIND = SUB + NORM_BEHIND
+GATE_PRODUCT_BEHIND = TURN_BEHIND + 1
+BACK_BEHIND = GATE_PRODUCT_BEHIND + H_TILES
 
 
 def tile_layernormlstmcell_pa_t_kernel(
@@ -43,163 +53,279 @@ def tile_layernormlstmcell_pa_t_kernel(
 ):
     nc = tc.nc
     weights = [
-        [(Wi_w_words, Wi_w_scales), (Ui_w_words, Ui_w_scales)],
-        [(Wc_w_words, Wc_w_scales), (Uc_w_words, Uc_w_scales)],
+        (Wi_w_words, Wi_w_scales),
+        (Ui_w_words, Ui_w_scales),
+        (Wc_w_words, Wc_w_scales),
+        (Uc_w_words, Uc_w_scales),
     ]
-    vectors = [(Wi_b, lni_g, lni_b), (Wc_b, lnc_g, lnc_b)]
+    biases = [Wi_b, Wc_b]
+    gains_shifts = [lni_g, lni_b, lnc_g, lnc_b]
     functions = [ACT.Sigmoid, ACT.Tanh]
 
-    with tc.tile_pool(name="const", bufs=1) as const, tc.tile_pool(
+    with tc.manual_schedule(), tc.tile_pool(name="const", bufs=1) as const, tc.tile_pool(
         name="rows", bufs=3
-    ) as rows, tc.tile_pool(name="quant", bufs=4) as quant, tc.tile_pool(
-        name="work", bufs=4
-    ) as work, tc.tile_pool(name="stat", bufs=8) as stat, tc.psum_pool(
-        name="psum_t", bufs=2
-    ) as psum_t, tc.psum_pool(name="psum_mm", bufs=4) as psum_mm:
-        planes = const.tile([P, H], U8, align_bytes=64)
-        nc.vector.memset(planes[:].bitcast(I32), 0)
-        ident = const.tile([P, P], F32)
-        make_identity(nc, ident[:])
-        neg_half = const.tile([P, 2], F32)
-        nc.vector.memset(neg_half[:], -0.5)
+    ) as rows, tc.tile_pool(name="quant", bufs=3) as quant, tc.tile_pool(
+        name="by_row", bufs=TURN_BEHIND + H_TILES + 2
+    ) as by_row, tc.tile_pool(name="by_feature", bufs=3) as by_feature, tc.tile_pool(
+        name="gate_products", bufs=2 * H_TILES + 1
+    ) as gate_products, tc.tile_pool(name="stat", bufs=4) as stat, tc.psum_pool(
+        name="psum", bufs=2
+    ) as psum:
+        x_blocks = {}
+        h_blocks = {}
 
-        w_words = []
-        for gate in range(2):
-            for operand in range(2):
-                words_in, scales_in = weights[gate][operand]
-                w = 2 * gate + operand
-                for quad in range(4):
-                    first = 32 * quad + 4 * w
-                    nc.sync.dma_start(
-                        out=planes[first : first + 4, :].bitcast(I32),
-                        in_=scales_in[0, 4 * quad : 4 * quad + 4, :].bitcast(I32),
-                    )
-                words = const.tile([P, H], U32, name="words%d" % w, align_bytes=64)
-                nc.sync.dma_start(
-                    out=words[:].bitcast(I32),
-                    in_=words_in[0].rearrange("p n t -> p (n t)").bitcast(I32),
-                )
-                w_words.append(words)
-
-        spread = []
-        for gate in range(2):
-            for v in range(3):
-                vec = const.tile([P, H], BF16, name="vec%d_%d" % (gate, v))
-                nc.sync.dma_start(out=vec[:], in_=vectors[gate][v].partition_broadcast(P))
-                spread.append(vec)
-
-        for block in range(N_BLOCKS):
+        def load(block):
             block_rows = slice(block * BLOCK, (block + 1) * BLOCK)
             x_sb = rows.tile([P, SUB, K], BF16)
-            nc.scalar.dma_start(
+            nc.sync.dma_start(
                 out=x_sb[:], in_=x[block_rows, :].rearrange("(p s) k -> p s k", s=SUB)
             )
             h_sb = rows.tile([P, SUB, K], BF16)
-            nc.scalar.dma_start(
+            nc.sync.dma_start(
                 out=h_sb[:], in_=h[block_rows, :].rearrange("(p s) k -> p s k", s=SUB)
             )
-            o_sb = rows.tile([P, SUB, H], F32)
+            x_blocks[block] = x_sb
+            h_blocks[block] = h_sb
 
-            for s in range(SUB):
-                flipped = psum_t.tile([P, 4, P], F32)
-                for operand, src in enumerate((x_sb, h_sb)):
-                    pairs = src[:, s, :].bitcast(F32)
-                    for u in range(2):
-                        nc.tensor.transpose(
-                            flipped[:, 2 * operand + u, :], pairs[:, u : K // 2 : 2], ident[:]
-                        )
-                grouped = quant.tile([P, 2 * P * 4], BF16, align_bytes=64)
-                nc.scalar.copy(
-                    out=grouped[:].bitcast(F32).rearrange("p (o r u) -> p o r u", o=2, u=2),
-                    in_=flipped[:].rearrange("p (o u) r -> p o r u", u=2),
-                )
-                codes = quant.tile([P, 2 * P], U32, align_bytes=64)
-                scales = quant.tile([P, 2 * P], U8, align_bytes=64)
-                nc.vector.quantize_mx(
-                    out=codes[:].bitcast(FP8X4), scales=scales[:], in_=grouped[:]
-                )
+        planes = const.tile([P, H], U8, align_bytes=64)
+        nc.vector.memset(planes[:].bitcast(I32), 0)
+        as_rows = const.tile([P, P], BF16)
+        nc.vector.memset(as_rows[:], 0.0)
+        neg_half = const.tile([P, GATES], F32)
+        nc.vector.memset(neg_half[:], -0.5)
+        ident = const.tile([P, P], F32)
+        make_identity(nc, ident[:])
+        ident_bf = const.tile([P, P], BF16)
+        make_identity(nc, ident_bf[:])
 
-                z_sum = stat.tile([P, 2], F32)
-                neg_mean = stat.tile([P, 2], F32)
-                sq_sum = stat.tile([P, 2], F32)
-                var_eps = stat.tile([P, 2], F32)
-                rstd = stat.tile([P, 2], F32)
-                z_gate = []
-                for gate in range(2):
-                    acc = psum_mm.tile([P, H], F32)
-                    for operand in range(2):
-                        w = 2 * gate + operand
-                        cols = slice(operand * P, (operand + 1) * P)
-                        nc.tensor.matmul_mx(
-                            out=acc[:],
-                            lhsT=codes[:, cols].bitcast(FP8X4),
-                            lhsT_scale=scales[:, cols],
-                            rhs=w_words[w][:].bitcast(FP8X4),
-                            rhs_scale=planes[4 * w : P, :],
-                            start=(operand == 0),
-                            stop=(operand == 1),
-                        )
-                    z = work.tile([P, H], F32, name="z%d" % gate)
-                    nc.vector.scalar_tensor_tensor(
-                        out=z[:],
-                        in0=acc[:],
-                        scalar=1.0,
-                        in1=spread[3 * gate][:],
-                        op0=ALU.mult,
-                        op1=ALU.add,
-                        accum_out=z_sum[:, gate : gate + 1],
-                    )
-                    z_gate.append(z)
-                nc.vector.tensor_scalar(
-                    out=neg_mean[:], in0=z_sum[:], scalar1=-1.0 / H, scalar2=None, op0=ALU.mult
-                )
-                for gate in range(2):
-                    squares = work.tile([P, H], BF16, name="squares%d" % gate)
-                    nc.scalar.activation(
-                        out=squares[:],
-                        in_=z_gate[gate][:],
-                        func=ACT.Square,
-                        bias=neg_mean[:, gate : gate + 1],
-                        scale=1.0,
-                        accum_out=sq_sum[:, gate : gate + 1],
-                    )
-                nc.vector.tensor_scalar(
-                    out=var_eps[:],
-                    in0=sq_sum[:],
-                    scalar1=1.0 / H,
-                    scalar2=EPS,
-                    op0=ALU.mult,
-                    op1=ALU.add,
-                )
-                nc.gpsimd.tensor_tensor(
-                    out=rstd[:], in0=var_eps[:], in1=neg_half[:], op=ALU.pow
-                )
-                acted = []
-                for gate in range(2):
-                    scaled = work.tile([P, H], F32, name="scaled%d" % gate)
-                    nc.vector.scalar_tensor_tensor(
-                        out=scaled[:],
-                        in0=z_gate[gate][:],
-                        scalar=neg_mean[:, gate : gate + 1],
-                        in1=spread[3 * gate + 1][:],
-                        op0=ALU.add,
-                        op1=ALU.mult,
-                    )
-                    shifted = work.tile([P, H], F32, name="shifted%d" % gate)
-                    nc.vector.scalar_tensor_tensor(
-                        out=shifted[:],
-                        in0=scaled[:],
-                        scalar=rstd[:, gate : gate + 1],
-                        in1=spread[3 * gate + 2][:],
-                        op0=ALU.mult,
-                        op1=ALU.add,
-                    )
-                    a = work.tile([P, H], F32, name="acted%d" % gate)
-                    nc.scalar.activation(out=a[:], in_=shifted[:], func=functions[gate])
-                    acted.append(a)
-                nc.vector.tensor_tensor(
-                    out=o_sb[:, s, :], in0=acted[0][:], in1=acted[1][:], op=ALU.mult
-                )
-            nc.sync.dma_start(
-                out=out[block_rows, :].rearrange("(p s) n -> p s n", s=SUB), in_=o_sb[:]
+        for v in range(2 * GATES):
+            nc.scalar.dma_start(
+                out=as_rows[H_TILES * v : H_TILES * (v + 1), :],
+                in_=gains_shifts[v].rearrange("(j f) -> j f", f=P),
             )
+        bias_rows = []
+        for gate in range(GATES):
+            bias_row = const.tile([P, H], BF16, name="bias_row%d" % gate)
+            nc.scalar.dma_start(out=bias_row[:], in_=biases[gate].partition_broadcast(P))
+            bias_rows.append(bias_row)
+
+        load(0)
+        for w in range(2 * GATES):
+            for quad in range(4):
+                first = 32 * quad + 4 * w
+                nc.sync.dma_start(
+                    out=planes[first : first + 4, :].bitcast(I32),
+                    in_=weights[w][1][0, 4 * quad : 4 * quad + 4, :].bitcast(I32),
+                )
+        w_words = []
+        for w in range(2 * GATES):
+            words = const.tile([P, H], U32, name="words%d" % w, align_bytes=64)
+            nc.sync.dma_start(
+                out=words[:].bitcast(I32),
+                in_=weights[w][0][0].rearrange("p n t -> p (n t)").bitcast(I32),
+            )
+            w_words.append(words)
+        load(1)
+
+        as_columns = psum.tile([P, P], BF16, tag="back")
+        nc.tensor.transpose(as_columns[:], as_rows[:], ident_bf[:])
+        affine = const.tile([P, 2 * GATES * H_TILES], F32)
+        nc.vector.tensor_copy(out=affine[:], in_=as_columns[:, 0 : 2 * GATES * H_TILES])
+
+        flipped = {}
+        grouped = {}
+        codes = {}
+        scales = {}
+        sums = {}
+        z = {}
+        stats = {}
+        acted = {}
+        gated = {}
+        o_blocks = {}
+
+        def flip(r):
+            block, s = divmod(r, SUB)
+            flipped[r] = psum.tile([P, 4, P], F32, name="flipped")
+            for operand, src in enumerate((x_blocks[block], h_blocks[block])):
+                pairs = src[:, s, :].bitcast(F32)
+                for u in range(2):
+                    nc.tensor.transpose(
+                        flipped[r][:, 2 * operand + u, :], pairs[:, u : K // 2 : 2], ident[:]
+                    )
+
+        def regroup(r):
+            grouped[r] = quant.tile([P, 2 * P * 4], BF16, name="grouped", align_bytes=64)
+            nc.vector.tensor_copy(
+                out=grouped[r][:].bitcast(F32).rearrange("p (o r u) -> p o r u", o=2, u=2),
+                in_=flipped[r][:].rearrange("p (o u) r -> p o r u", u=2),
+            )
+
+        def quantise(r):
+            codes[r] = quant.tile([P, 2 * P], U32, name="codes", align_bytes=64)
+            scales[r] = quant.tile([P, 2 * P], U8, name="scales", align_bytes=64)
+            nc.vector.quantize_mx(
+                out=codes[r][:].bitcast(FP8X4), scales=scales[r][:], in_=grouped[r][:]
+            )
+
+        def multiply(r, gate):
+            sums[r, gate] = psum.tile([P, H], F32, name="sums")
+            for operand in range(2):
+                w = 2 * gate + operand
+                cols = slice(operand * P, (operand + 1) * P)
+                nc.tensor.matmul_mx(
+                    out=sums[r, gate][:],
+                    lhsT=codes[r][:, cols].bitcast(FP8X4),
+                    lhsT_scale=scales[r][:, cols],
+                    rhs=w_words[w][:].bitcast(FP8X4),
+                    rhs_scale=planes[4 * w : P, :],
+                    start=(operand == 0),
+                    stop=(operand == 1),
+                )
+
+        def add_bias(r, gate):
+            if gate == 0:
+                stats[r] = [
+                    stat.tile([P, GATES], F32, name="stat%d" % i) for i in range(5)
+                ]
+            z[r, gate] = by_row.tile([P, H], F32, name="z%d" % gate)
+            nc.vector.scalar_tensor_tensor(
+                out=z[r, gate][:],
+                in0=sums[r, gate][:],
+                scalar=1.0,
+                in1=bias_rows[gate][:],
+                op0=ALU.mult,
+                op1=ALU.add,
+                accum_out=stats[r][0][:, gate : gate + 1],
+            )
+
+        def mean(r):
+            z_sum, neg_mean = stats[r][0], stats[r][1]
+            nc.vector.tensor_scalar(
+                out=neg_mean[:], in0=z_sum[:], scalar1=-1.0 / H, scalar2=None, op0=ALU.mult
+            )
+
+        def squares(r, gate):
+            neg_mean, sq_sum = stats[r][1], stats[r][2]
+            unused = by_feature.tile([P, H], BF16, name="unused%d" % gate)
+            nc.scalar.activation(
+                out=unused[:],
+                in_=z[r, gate][:],
+                func=ACT.Square,
+                bias=neg_mean[:, gate : gate + 1],
+                scale=1.0,
+                accum_out=sq_sum[:, gate : gate + 1],
+            )
+
+        def inverse_std(r):
+            sq_sum, var_eps, rstd = stats[r][2], stats[r][3], stats[r][4]
+            nc.gpsimd.tensor_scalar(
+                out=var_eps[:],
+                in0=sq_sum[:],
+                scalar1=1.0 / H,
+                scalar2=EPS,
+                op0=ALU.mult,
+                op1=ALU.add,
+            )
+            nc.gpsimd.tensor_tensor(out=rstd[:], in0=var_eps[:], in1=neg_half[:], op=ALU.pow)
+
+        def normalise(r, gate):
+            neg_mean, rstd = stats[r][1], stats[r][4]
+            nc.vector.tensor_scalar(
+                out=z[r, gate][:],
+                in0=z[r, gate][:],
+                scalar1=neg_mean[:, gate : gate + 1],
+                scalar2=rstd[:, gate : gate + 1],
+                op0=ALU.add,
+                op1=ALU.mult,
+            )
+
+        turned = {}
+
+        def turn(block, j, gate):
+            turned[block, j, gate] = psum.tile([P, SUB, P], F32, name="turned")
+            for s in range(SUB):
+                nc.tensor.transpose(
+                    turned[block, j, gate][:, s, :],
+                    z[block * SUB + s, gate][:, j * P : (j + 1) * P],
+                    ident[:],
+                )
+
+        def activate(block, j, gate):
+            acted[block, j, gate] = by_feature.tile([P, SUB, P], F32, name="acted%d" % gate)
+            gain = (2 * gate) * H_TILES + j
+            shift = (2 * gate + 1) * H_TILES + j
+            nc.scalar.activation(
+                out=acted[block, j, gate][:],
+                in_=turned[block, j, gate][:],
+                func=functions[gate],
+                bias=affine[:, shift : shift + 1],
+                scale=affine[:, gain : gain + 1],
+            )
+
+        def gate_product(block, j):
+            gated[block, j] = gate_products.tile([P, SUB, P], F32, name="gated")
+            nc.gpsimd.tensor_tensor(
+                out=gated[block, j][:],
+                in0=acted[block, j, 0][:],
+                in1=acted[block, j, 1][:],
+                op=ALU.mult,
+            )
+
+        back = {}
+
+        def turn_back(r):
+            block, s = divmod(r, SUB)
+            back[r] = psum.tile([P, H_TILES, P], F32, name="back")
+            for j in range(H_TILES):
+                nc.tensor.transpose(back[r][:, j, :], gated[block, j][:, s, :], ident[:])
+
+        def leave(r):
+            block, s = divmod(r, SUB)
+            if s == 0:
+                o_blocks[block] = rows.tile([P, SUB, H], F32, name="o_sb")
+            nc.scalar.copy(
+                out=o_blocks[block][:, s, :], in_=back[r][:].rearrange("p j f -> p (j f)")
+            )
+            if s == SUB - 1:
+                block_rows = slice(block * BLOCK, (block + 1) * BLOCK)
+                nc.sync.dma_start(
+                    out=out[block_rows, :].rearrange("(p s) n -> p s n", s=SUB),
+                    in_=o_blocks[block][:],
+                )
+
+        def is_tile(r):
+            return 0 <= r < N_TILES
+
+        for step in range(-FLIP_AHEAD, N_TILES + BACK_BEHIND):
+            if step % SUB == 0 and 0 <= step // SUB + 2 < N_BLOCKS:
+                load(step // SUB + 2)
+            if is_tile(step):
+                multiply(step, 0)
+                multiply(step, 1)
+            if is_tile(step - GATE_PRODUCT_BEHIND):
+                gate_product(*divmod(step - GATE_PRODUCT_BEHIND, H_TILES))
+            if is_tile(step + QUANT_AHEAD):
+                regroup(step + QUANT_AHEAD)
+            if is_tile(step - NORM_BEHIND):
+                squares(step - NORM_BEHIND, 0)
+                squares(step - NORM_BEHIND, 1)
+                inverse_std(step - NORM_BEHIND)
+            if is_tile(step):
+                add_bias(step, 0)
+                add_bias(step, 1)
+                mean(step)
+            if is_tile(step + QUANT_AHEAD):
+                quantise(step + QUANT_AHEAD)
+            if is_tile(step - NORM_BEHIND):
+                normalise(step - NORM_BEHIND, 0)
+                normalise(step - NORM_BEHIND, 1)
+            if is_tile(step - TURN_BEHIND):
+                block, j = divmod(step - TURN_BEHIND, H_TILES)
+                for gate in range(GATES):
+                    turn(block, j, gate)
+                    activate(block, j, gate)
+            if is_tile(step - BACK_BEHIND):
+                turn_back(step - BACK_BEHIND)
+                leave(step - BACK_BEHIND)
+            if is_tile(step + FLIP_AHEAD):
+                flip(step + FLIP_AHEAD)

@@ -16,19 +16,23 @@ K = 512
 H = 512
 H_TILES = H // P
 EPS = 1e-5
-SUB = 4
-BLOCK = P * SUB
-N_BLOCKS = B // BLOCK
 N_TILES = B // P
+GROUP = 4
 GATES = 2
 FLOPS = 2 * B * (2 * K) * (GATES * H)
 
-FLIP_AHEAD = 2
+LOAD_AHEAD = 6
+FLIP_AHEAD = 3
+REGROUP_AHEAD = 2
 QUANT_AHEAD = 1
-NORM_BEHIND = 1
-TURN_BEHIND = SUB + NORM_BEHIND
+MEAN_BEHIND = 1
+SQUARES_BEHIND = 2
+STD_BEHIND = 3
+NORM_BEHIND = 4
+TURN_BEHIND = GROUP + NORM_BEHIND
 GATE_PRODUCT_BEHIND = TURN_BEHIND + 1
 BACK_BEHIND = GATE_PRODUCT_BEHIND + H_TILES
+LEAVE_BEHIND = BACK_BEHIND + 1
 
 
 def tile_layernormlstmcell_pa_t_kernel(
@@ -63,29 +67,181 @@ def tile_layernormlstmcell_pa_t_kernel(
     functions = [ACT.Sigmoid, ACT.Tanh]
 
     with tc.manual_schedule(), tc.tile_pool(name="const", bufs=1) as const, tc.tile_pool(
-        name="rows", bufs=3
+        name="rows", bufs=LOAD_AHEAD - FLIP_AHEAD + 2
     ) as rows, tc.tile_pool(name="quant", bufs=3) as quant, tc.tile_pool(
-        name="by_row", bufs=TURN_BEHIND + H_TILES + 2
+        name="by_row", bufs=TURN_BEHIND + H_TILES
     ) as by_row, tc.tile_pool(name="by_feature", bufs=3) as by_feature, tc.tile_pool(
         name="gate_products", bufs=2 * H_TILES + 1
-    ) as gate_products, tc.tile_pool(name="stat", bufs=4) as stat, tc.psum_pool(
+    ) as gate_products, tc.tile_pool(name="stat", bufs=NORM_BEHIND + 2) as stat, tc.psum_pool(
         name="psum", bufs=2
     ) as psum:
-        x_blocks = {}
-        h_blocks = {}
+        x_rows = {}
+        h_rows = {}
+        flipped = {}
+        grouped = {}
+        codes = {}
+        scales = {}
+        sums = {}
+        z = {}
+        stats = {}
+        turned = {}
+        acted = {}
+        gated = {}
+        back = {}
 
-        def load(block):
-            block_rows = slice(block * BLOCK, (block + 1) * BLOCK)
-            x_sb = rows.tile([P, SUB, K], BF16)
-            nc.sync.dma_start(
-                out=x_sb[:], in_=x[block_rows, :].rearrange("(p s) k -> p s k", s=SUB)
+        def load(r):
+            tile_rows = slice(r * P, (r + 1) * P)
+            x_rows[r] = rows.tile([P, K], BF16, name="x_rows")
+            nc.sync.dma_start(out=x_rows[r][:], in_=x[tile_rows, :])
+            h_rows[r] = rows.tile([P, K], BF16, name="h_rows")
+            nc.sync.dma_start(out=h_rows[r][:], in_=h[tile_rows, :])
+
+        def flip(r):
+            flipped[r] = psum.tile([P, 4, P], F32, name="flipped")
+            for operand, src in enumerate((x_rows[r], h_rows[r])):
+                pairs = src[:].bitcast(F32)
+                for u in range(2):
+                    nc.tensor.transpose(
+                        flipped[r][:, 2 * operand + u, :], pairs[:, u : K // 2 : 2], ident[:]
+                    )
+
+        def regroup(r):
+            grouped[r] = quant.tile([P, 2 * P * 4], BF16, name="grouped", align_bytes=64)
+            nc.scalar.copy(
+                out=grouped[r][:].bitcast(F32).rearrange("p (o r u) -> p o r u", o=2, u=2),
+                in_=flipped[r][:].rearrange("p (o u) r -> p o r u", u=2),
             )
-            h_sb = rows.tile([P, SUB, K], BF16)
-            nc.sync.dma_start(
-                out=h_sb[:], in_=h[block_rows, :].rearrange("(p s) k -> p s k", s=SUB)
+
+        def quantise(r):
+            codes[r] = quant.tile([P, 2 * P], U32, name="codes", align_bytes=64)
+            scales[r] = quant.tile([P, 2 * P], U8, name="scales", align_bytes=64)
+            nc.vector.quantize_mx(
+                out=codes[r][:].bitcast(FP8X4), scales=scales[r][:], in_=grouped[r][:]
             )
-            x_blocks[block] = x_sb
-            h_blocks[block] = h_sb
+
+        def multiply(r, gate):
+            sums[r, gate] = psum.tile([P, H], F32, name="sums")
+            for operand in range(2):
+                w = 2 * gate + operand
+                cols = slice(operand * P, (operand + 1) * P)
+                nc.tensor.matmul_mx(
+                    out=sums[r, gate][:],
+                    lhsT=codes[r][:, cols].bitcast(FP8X4),
+                    lhsT_scale=scales[r][:, cols],
+                    rhs=w_words[w][:].bitcast(FP8X4),
+                    rhs_scale=planes[4 * w : P, :],
+                    start=(operand == 0),
+                    stop=(operand == 1),
+                )
+
+        def add_bias(r, gate):
+            if gate == 0:
+                stats[r] = [stat.tile([P, GATES], F32, name="stat%d" % i) for i in range(5)]
+            z[r, gate] = by_row.tile([P, H], F32, name="z%d" % gate)
+            nc.vector.scalar_tensor_tensor(
+                out=z[r, gate][:],
+                in0=sums[r, gate][:],
+                scalar=1.0,
+                in1=bias_rows[gate][:],
+                op0=ALU.mult,
+                op1=ALU.add,
+                accum_out=stats[r][0][:, gate : gate + 1],
+            )
+
+        def mean(r):
+            z_sum, neg_mean = stats[r][0], stats[r][1]
+            nc.gpsimd.tensor_scalar(
+                out=neg_mean[:],
+                in0=z_sum[:],
+                scalar1=-1.0 / H,
+                scalar2=0.0,
+                op0=ALU.mult,
+                op1=ALU.add,
+            )
+
+        def squares(r, gate):
+            neg_mean, sq_sum = stats[r][1], stats[r][2]
+            unused = by_feature.tile([P, H], BF16, name="unused%d" % gate)
+            nc.scalar.activation(
+                out=unused[:],
+                in_=z[r, gate][:],
+                func=ACT.Square,
+                bias=neg_mean[:, gate : gate + 1],
+                scale=1.0,
+                accum_out=sq_sum[:, gate : gate + 1],
+            )
+
+        def inverse_std(r):
+            sq_sum, var_eps, rstd = stats[r][2], stats[r][3], stats[r][4]
+            nc.gpsimd.tensor_scalar(
+                out=var_eps[:],
+                in0=sq_sum[:],
+                scalar1=1.0 / H,
+                scalar2=EPS,
+                op0=ALU.mult,
+                op1=ALU.add,
+            )
+            nc.gpsimd.tensor_tensor(out=rstd[:], in0=var_eps[:], in1=neg_half[:], op=ALU.pow)
+
+        def normalise(r, gate):
+            neg_mean, rstd = stats[r][1], stats[r][4]
+            nc.vector.tensor_scalar(
+                out=z[r, gate][:],
+                in0=z[r, gate][:],
+                scalar1=neg_mean[:, gate : gate + 1],
+                scalar2=rstd[:, gate : gate + 1],
+                op0=ALU.add,
+                op1=ALU.mult,
+            )
+
+        def turn(group, j, gate):
+            turned[group, j, gate] = psum.tile([P, GROUP, P], F32, name="turned")
+            for s in range(GROUP):
+                nc.tensor.transpose(
+                    turned[group, j, gate][:, s, :],
+                    z[group * GROUP + s, gate][:, j * P : (j + 1) * P],
+                    ident[:],
+                )
+
+        def activate(group, j, gate):
+            acted[group, j, gate] = by_feature.tile([P, GROUP, P], F32, name="acted%d" % gate)
+            gain = (2 * gate) * H_TILES + j
+            shift = (2 * gate + 1) * H_TILES + j
+            nc.scalar.activation(
+                out=acted[group, j, gate][:],
+                in_=turned[group, j, gate][:],
+                func=functions[gate],
+                bias=affine[:, shift : shift + 1],
+                scale=affine[:, gain : gain + 1],
+            )
+
+        def gate_product(group, j):
+            gated[group, j] = gate_products.tile([P, GROUP, P], F32, name="gated")
+            nc.vector.tensor_tensor(
+                out=gated[group, j][:],
+                in0=acted[group, j, 0][:],
+                in1=acted[group, j, 1][:],
+                op=ALU.mult,
+            )
+
+        def turn_back(r):
+            group, s = divmod(r, GROUP)
+            back[r] = psum.tile([P, H_TILES, P], F32, name="back")
+            for j in range(H_TILES):
+                nc.tensor.transpose(back[r][:, j, :], gated[group, j][:, s, :], ident[:])
+
+        def leave(r):
+            result = rows.tile([P, H], F32, name="result")
+            if r % 2 == 0:
+                nc.scalar.copy(out=result[:], in_=back[r][:].rearrange("p j f -> p (j f)"))
+            else:
+                nc.vector.tensor_copy(
+                    out=result[:], in_=back[r][:].rearrange("p j f -> p (j f)")
+                )
+            nc.sync.dma_start(out=out[r * P : (r + 1) * P, :], in_=result[:])
+
+        def is_tile(r):
+            return 0 <= r < N_TILES
 
         planes = const.tile([P, H], U8, align_bytes=64)
         nc.vector.memset(planes[:].bitcast(I32), 0)
@@ -125,207 +281,48 @@ def tile_layernormlstmcell_pa_t_kernel(
                 in_=weights[w][0][0].rearrange("p n t -> p (n t)").bitcast(I32),
             )
             w_words.append(words)
-        load(1)
+        for r in range(1, LOAD_AHEAD - FLIP_AHEAD):
+            load(r)
 
         as_columns = psum.tile([P, P], BF16, tag="back")
         nc.tensor.transpose(as_columns[:], as_rows[:], ident_bf[:])
         affine = const.tile([P, 2 * GATES * H_TILES], F32)
         nc.vector.tensor_copy(out=affine[:], in_=as_columns[:, 0 : 2 * GATES * H_TILES])
 
-        flipped = {}
-        grouped = {}
-        codes = {}
-        scales = {}
-        sums = {}
-        z = {}
-        stats = {}
-        acted = {}
-        gated = {}
-        o_blocks = {}
-
-        def flip(r):
-            block, s = divmod(r, SUB)
-            flipped[r] = psum.tile([P, 4, P], F32, name="flipped")
-            for operand, src in enumerate((x_blocks[block], h_blocks[block])):
-                pairs = src[:, s, :].bitcast(F32)
-                for u in range(2):
-                    nc.tensor.transpose(
-                        flipped[r][:, 2 * operand + u, :], pairs[:, u : K // 2 : 2], ident[:]
-                    )
-
-        def regroup(r):
-            grouped[r] = quant.tile([P, 2 * P * 4], BF16, name="grouped", align_bytes=64)
-            nc.vector.tensor_copy(
-                out=grouped[r][:].bitcast(F32).rearrange("p (o r u) -> p o r u", o=2, u=2),
-                in_=flipped[r][:].rearrange("p (o u) r -> p o r u", u=2),
-            )
-
-        def quantise(r):
-            codes[r] = quant.tile([P, 2 * P], U32, name="codes", align_bytes=64)
-            scales[r] = quant.tile([P, 2 * P], U8, name="scales", align_bytes=64)
-            nc.vector.quantize_mx(
-                out=codes[r][:].bitcast(FP8X4), scales=scales[r][:], in_=grouped[r][:]
-            )
-
-        def multiply(r, gate):
-            sums[r, gate] = psum.tile([P, H], F32, name="sums")
-            for operand in range(2):
-                w = 2 * gate + operand
-                cols = slice(operand * P, (operand + 1) * P)
-                nc.tensor.matmul_mx(
-                    out=sums[r, gate][:],
-                    lhsT=codes[r][:, cols].bitcast(FP8X4),
-                    lhsT_scale=scales[r][:, cols],
-                    rhs=w_words[w][:].bitcast(FP8X4),
-                    rhs_scale=planes[4 * w : P, :],
-                    start=(operand == 0),
-                    stop=(operand == 1),
-                )
-
-        def add_bias(r, gate):
-            if gate == 0:
-                stats[r] = [
-                    stat.tile([P, GATES], F32, name="stat%d" % i) for i in range(5)
-                ]
-            z[r, gate] = by_row.tile([P, H], F32, name="z%d" % gate)
-            nc.vector.scalar_tensor_tensor(
-                out=z[r, gate][:],
-                in0=sums[r, gate][:],
-                scalar=1.0,
-                in1=bias_rows[gate][:],
-                op0=ALU.mult,
-                op1=ALU.add,
-                accum_out=stats[r][0][:, gate : gate + 1],
-            )
-
-        def mean(r):
-            z_sum, neg_mean = stats[r][0], stats[r][1]
-            nc.vector.tensor_scalar(
-                out=neg_mean[:], in0=z_sum[:], scalar1=-1.0 / H, scalar2=None, op0=ALU.mult
-            )
-
-        def squares(r, gate):
-            neg_mean, sq_sum = stats[r][1], stats[r][2]
-            unused = by_feature.tile([P, H], BF16, name="unused%d" % gate)
-            nc.scalar.activation(
-                out=unused[:],
-                in_=z[r, gate][:],
-                func=ACT.Square,
-                bias=neg_mean[:, gate : gate + 1],
-                scale=1.0,
-                accum_out=sq_sum[:, gate : gate + 1],
-            )
-
-        def inverse_std(r):
-            sq_sum, var_eps, rstd = stats[r][2], stats[r][3], stats[r][4]
-            nc.gpsimd.tensor_scalar(
-                out=var_eps[:],
-                in0=sq_sum[:],
-                scalar1=1.0 / H,
-                scalar2=EPS,
-                op0=ALU.mult,
-                op1=ALU.add,
-            )
-            nc.gpsimd.tensor_tensor(out=rstd[:], in0=var_eps[:], in1=neg_half[:], op=ALU.pow)
-
-        def normalise(r, gate):
-            neg_mean, rstd = stats[r][1], stats[r][4]
-            nc.vector.tensor_scalar(
-                out=z[r, gate][:],
-                in0=z[r, gate][:],
-                scalar1=neg_mean[:, gate : gate + 1],
-                scalar2=rstd[:, gate : gate + 1],
-                op0=ALU.add,
-                op1=ALU.mult,
-            )
-
-        turned = {}
-
-        def turn(block, j, gate):
-            turned[block, j, gate] = psum.tile([P, SUB, P], F32, name="turned")
-            for s in range(SUB):
-                nc.tensor.transpose(
-                    turned[block, j, gate][:, s, :],
-                    z[block * SUB + s, gate][:, j * P : (j + 1) * P],
-                    ident[:],
-                )
-
-        def activate(block, j, gate):
-            acted[block, j, gate] = by_feature.tile([P, SUB, P], F32, name="acted%d" % gate)
-            gain = (2 * gate) * H_TILES + j
-            shift = (2 * gate + 1) * H_TILES + j
-            nc.scalar.activation(
-                out=acted[block, j, gate][:],
-                in_=turned[block, j, gate][:],
-                func=functions[gate],
-                bias=affine[:, shift : shift + 1],
-                scale=affine[:, gain : gain + 1],
-            )
-
-        def gate_product(block, j):
-            gated[block, j] = gate_products.tile([P, SUB, P], F32, name="gated")
-            nc.gpsimd.tensor_tensor(
-                out=gated[block, j][:],
-                in0=acted[block, j, 0][:],
-                in1=acted[block, j, 1][:],
-                op=ALU.mult,
-            )
-
-        back = {}
-
-        def turn_back(r):
-            block, s = divmod(r, SUB)
-            back[r] = psum.tile([P, H_TILES, P], F32, name="back")
-            for j in range(H_TILES):
-                nc.tensor.transpose(back[r][:, j, :], gated[block, j][:, s, :], ident[:])
-
-        def leave(r):
-            block, s = divmod(r, SUB)
-            if s == 0:
-                o_blocks[block] = rows.tile([P, SUB, H], F32, name="o_sb")
-            nc.scalar.copy(
-                out=o_blocks[block][:, s, :], in_=back[r][:].rearrange("p j f -> p (j f)")
-            )
-            if s == SUB - 1:
-                block_rows = slice(block * BLOCK, (block + 1) * BLOCK)
-                nc.sync.dma_start(
-                    out=out[block_rows, :].rearrange("(p s) n -> p s n", s=SUB),
-                    in_=o_blocks[block][:],
-                )
-
-        def is_tile(r):
-            return 0 <= r < N_TILES
-
-        for step in range(-FLIP_AHEAD, N_TILES + BACK_BEHIND):
-            if step % SUB == 0 and 0 <= step // SUB + 2 < N_BLOCKS:
-                load(step // SUB + 2)
+        for step in range(-FLIP_AHEAD, N_TILES + LEAVE_BEHIND):
+            if is_tile(step + LOAD_AHEAD):
+                load(step + LOAD_AHEAD)
             if is_tile(step):
                 multiply(step, 0)
-                multiply(step, 1)
-            if is_tile(step - GATE_PRODUCT_BEHIND):
-                gate_product(*divmod(step - GATE_PRODUCT_BEHIND, H_TILES))
-            if is_tile(step + QUANT_AHEAD):
-                regroup(step + QUANT_AHEAD)
-            if is_tile(step - NORM_BEHIND):
-                squares(step - NORM_BEHIND, 0)
-                squares(step - NORM_BEHIND, 1)
-                inverse_std(step - NORM_BEHIND)
+            if is_tile(step - LEAVE_BEHIND):
+                leave(step - LEAVE_BEHIND)
+            if is_tile(step - STD_BEHIND):
+                inverse_std(step - STD_BEHIND)
+            if is_tile(step - MEAN_BEHIND):
+                mean(step - MEAN_BEHIND)
             if is_tile(step):
                 add_bias(step, 0)
-                add_bias(step, 1)
-                mean(step)
+            if is_tile(step - TURN_BEHIND):
+                group, j = divmod(step - TURN_BEHIND, H_TILES)
+                for gate in range(GATES):
+                    turn(group, j, gate)
+                    activate(group, j, gate)
+            if is_tile(step + REGROUP_AHEAD):
+                regroup(step + REGROUP_AHEAD)
             if is_tile(step + QUANT_AHEAD):
                 quantise(step + QUANT_AHEAD)
+            if is_tile(step - GATE_PRODUCT_BEHIND):
+                gate_product(*divmod(step - GATE_PRODUCT_BEHIND, H_TILES))
+            if is_tile(step):
+                multiply(step, 1)
+                add_bias(step, 1)
+            if is_tile(step - SQUARES_BEHIND):
+                squares(step - SQUARES_BEHIND, 0)
+                squares(step - SQUARES_BEHIND, 1)
             if is_tile(step - NORM_BEHIND):
                 normalise(step - NORM_BEHIND, 0)
                 normalise(step - NORM_BEHIND, 1)
-            if is_tile(step - TURN_BEHIND):
-                block, j = divmod(step - TURN_BEHIND, H_TILES)
-                for gate in range(GATES):
-                    turn(block, j, gate)
-                    activate(block, j, gate)
             if is_tile(step - BACK_BEHIND):
                 turn_back(step - BACK_BEHIND)
-                leave(step - BACK_BEHIND)
             if is_tile(step + FLIP_AHEAD):
                 flip(step + FLIP_AHEAD)

@@ -31,6 +31,7 @@ STD_BEHIND = 3
 NORM_BEHIND = 4
 TURN_BEHIND = GROUP + NORM_BEHIND
 GATE_PRODUCT_BEHIND = TURN_BEHIND + 1
+AFFINE_STEP = TURN_BEHIND - 2
 BACK_BEHIND = GATE_PRODUCT_BEHIND + H_TILES
 LEAVE_BEHIND = BACK_BEHIND + 1
 
@@ -245,6 +246,10 @@ def tile_layernormlstmcell_pa_t_kernel(
 
         planes = const.tile([P, H], U8, align_bytes=64)
         nc.vector.memset(planes[:].bitcast(I32), 0)
+        bias_in_row_0 = const.tile([P, GATES, H], BF16)
+        nc.vector.memset(bias_in_row_0[:], 0.0)
+        ones = const.tile([P, P], BF16)
+        nc.vector.memset(ones[:], 1.0)
         as_rows = const.tile([P, P], BF16)
         nc.vector.memset(as_rows[:], 0.0)
         neg_half = const.tile([P, GATES], F32)
@@ -254,18 +259,12 @@ def tile_layernormlstmcell_pa_t_kernel(
         ident_bf = const.tile([P, P], BF16)
         make_identity(nc, ident_bf[:])
 
-        for v in range(2 * GATES):
-            nc.scalar.dma_start(
-                out=as_rows[H_TILES * v : H_TILES * (v + 1), :],
-                in_=gains_shifts[v].rearrange("(j f) -> j f", f=P),
-            )
-        bias_rows = []
-        for gate in range(GATES):
-            bias_row = const.tile([P, H], BF16, name="bias_row%d" % gate)
-            nc.scalar.dma_start(out=bias_row[:], in_=biases[gate].partition_broadcast(P))
-            bias_rows.append(bias_row)
-
         load(0)
+        for gate in range(GATES):
+            nc.sync.dma_start(
+                out=bias_in_row_0[0:1, gate, :], in_=biases[gate].rearrange("(o n) -> o n", o=1)
+            )
+        w_words = []
         for w in range(2 * GATES):
             for quad in range(4):
                 first = 32 * quad + 4 * w
@@ -273,23 +272,42 @@ def tile_layernormlstmcell_pa_t_kernel(
                     out=planes[first : first + 4, :].bitcast(I32),
                     in_=weights[w][1][0, 4 * quad : 4 * quad + 4, :].bitcast(I32),
                 )
-        w_words = []
-        for w in range(2 * GATES):
-            words = const.tile([P, H], U32, name="words%d" % w, align_bytes=64)
-            nc.sync.dma_start(
-                out=words[:].bitcast(I32),
-                in_=weights[w][0][0].rearrange("p n t -> p (n t)").bitcast(I32),
-            )
-            w_words.append(words)
+            if w % 2 == 1:
+                for loaded in (w - 1, w):
+                    words = const.tile([P, H], U32, name="words%d" % loaded, align_bytes=64)
+                    nc.sync.dma_start(
+                        out=words[:].bitcast(I32),
+                        in_=weights[loaded][0][0].rearrange("p n t -> p (n t)").bitcast(I32),
+                    )
+                    w_words.append(words)
         for r in range(1, LOAD_AHEAD - FLIP_AHEAD):
             load(r)
 
-        as_columns = psum.tile([P, P], BF16, tag="back")
-        nc.tensor.transpose(as_columns[:], as_rows[:], ident_bf[:])
+        bias_rows = []
+        for gate in range(GATES):
+            repeated = psum.tile([P, H], F32, tag="sums")
+            nc.tensor.matmul(
+                out=repeated[:], lhsT=ones[:], rhs=bias_in_row_0[:, gate, :], start=True, stop=True
+            )
+            bias_row = const.tile([P, H], F32, name="bias_row%d" % gate)
+            nc.vector.tensor_copy(out=bias_row[:], in_=repeated[:])
+            bias_rows.append(bias_row)
+
+        for v in range(2 * GATES):
+            nc.sync.dma_start(
+                out=as_rows[H_TILES * v : H_TILES * (v + 1), :],
+                in_=gains_shifts[v].rearrange("(j f) -> j f", f=P),
+            )
         affine = const.tile([P, 2 * GATES * H_TILES], F32)
-        nc.vector.tensor_copy(out=affine[:], in_=as_columns[:, 0 : 2 * GATES * H_TILES])
+
+        def prepare_affine():
+            as_columns = psum.tile([P, P], BF16, tag="back")
+            nc.tensor.transpose(as_columns[:], as_rows[:], ident_bf[:])
+            nc.vector.tensor_copy(out=affine[:], in_=as_columns[:, 0 : 2 * GATES * H_TILES])
 
         for step in range(-FLIP_AHEAD, N_TILES + LEAVE_BEHIND):
+            if step == AFFINE_STEP:
+                prepare_affine()
             if is_tile(step + LOAD_AHEAD):
                 load(step + LOAD_AHEAD)
             if is_tile(step):

@@ -233,13 +233,20 @@ def tile_layernormlstmcell_pa_t_kernel(
 
         def leave(r):
             result = rows.tile([P, H], F32, name="result")
-            if r % 2 == 0:
+            if r % 2 == 0 and (r + LEAVE_BEHIND < N_TILES or r >= N_TILES - GROUP):
                 nc.scalar.copy(out=result[:], in_=back[r][:].rearrange("p j f -> p (j f)"))
             else:
                 nc.vector.tensor_copy(
                     out=result[:], in_=back[r][:].rearrange("p j f -> p (j f)")
                 )
             nc.sync.dma_start(out=out[r * P : (r + 1) * P, :], in_=result[:])
+
+        def keep_clock():
+            idle = psum.tile([P, H], F32, tag="sums")
+            for gate in range(GATES):
+                nc.tensor.matmul(
+                    out=idle[:], lhsT=ones[:], rhs=bias_in_row_0[:, gate, :], start=True, stop=True
+                )
 
         def is_tile(r):
             return 0 <= r < N_TILES
@@ -312,6 +319,8 @@ def tile_layernormlstmcell_pa_t_kernel(
                 load(step + LOAD_AHEAD)
             if is_tile(step):
                 multiply(step, 0)
+            elif is_tile(step - TURN_BEHIND):
+                keep_clock()
             if is_tile(step - LEAVE_BEHIND):
                 leave(step - LEAVE_BEHIND)
             if is_tile(step - STD_BEHIND):

@@ -21,6 +21,7 @@ GROUP = 4
 GATES = 2
 FLOPS = 2 * B * (2 * K) * (GATES * H)
 
+FIRST_TILES = 3
 LOAD_AHEAD = 6
 FLIP_AHEAD = 3
 REGROUP_AHEAD = 2
@@ -255,6 +256,10 @@ def tile_layernormlstmcell_pa_t_kernel(
         nc.vector.memset(planes[:].bitcast(I32), 0)
         bias_in_row_0 = const.tile([P, GATES, H], BF16)
         nc.vector.memset(bias_in_row_0[:], 0.0)
+        for gate in range(GATES):
+            nc.gpsimd.dma_start(
+                out=bias_in_row_0[0:1, gate, :], in_=biases[gate].rearrange("(o n) -> o n", o=1)
+            )
         ones = const.tile([P, P], BF16)
         nc.vector.memset(ones[:], 1.0)
         as_rows = const.tile([P, P], BF16)
@@ -266,11 +271,15 @@ def tile_layernormlstmcell_pa_t_kernel(
         ident_bf = const.tile([P, P], BF16)
         make_identity(nc, ident_bf[:])
 
-        load(0)
-        for gate in range(GATES):
+        first_x = const.tile([P, FIRST_TILES, K], BF16)
+        first_h = const.tile([P, FIRST_TILES, K], BF16)
+        for first, operand in ((first_x, x), (first_h, h)):
             nc.sync.dma_start(
-                out=bias_in_row_0[0:1, gate, :], in_=biases[gate].rearrange("(o n) -> o n", o=1)
+                out=first[:], in_=operand[0 : FIRST_TILES * P, :].rearrange("(s p) k -> p s k", p=P)
             )
+        for r in range(FIRST_TILES):
+            x_rows[r] = first_x[:, r, :]
+            h_rows[r] = first_h[:, r, :]
         w_words = []
         for w in range(2 * GATES):
             for quad in range(4):
@@ -287,21 +296,25 @@ def tile_layernormlstmcell_pa_t_kernel(
                         in_=weights[loaded][0][0].rearrange("p n t -> p (n t)").bitcast(I32),
                     )
                     w_words.append(words)
-        for r in range(1, LOAD_AHEAD - FLIP_AHEAD):
-            load(r)
 
         bias_rows = []
-        for gate in range(GATES):
-            repeated = psum.tile([P, H], F32, tag="sums")
-            nc.tensor.matmul(
-                out=repeated[:], lhsT=ones[:], rhs=bias_in_row_0[:, gate, :], start=True, stop=True
-            )
-            bias_row = const.tile([P, H], F32, name="bias_row%d" % gate)
-            nc.vector.tensor_copy(out=bias_row[:], in_=repeated[:])
-            bias_rows.append(bias_row)
+
+        def spread_biases():
+            for gate in range(GATES):
+                repeated = psum.tile([P, H], F32, tag="sums")
+                nc.tensor.matmul(
+                    out=repeated[:],
+                    lhsT=ones[:],
+                    rhs=bias_in_row_0[:, gate, :],
+                    start=True,
+                    stop=True,
+                )
+                bias_row = const.tile([P, H], F32, name="bias_row%d" % gate)
+                nc.vector.tensor_copy(out=bias_row[:], in_=repeated[:])
+                bias_rows.append(bias_row)
 
         for v in range(2 * GATES):
-            nc.sync.dma_start(
+            nc.gpsimd.dma_start(
                 out=as_rows[H_TILES * v : H_TILES * (v + 1), :],
                 in_=gains_shifts[v].rearrange("(j f) -> j f", f=P),
             )
@@ -313,6 +326,8 @@ def tile_layernormlstmcell_pa_t_kernel(
             nc.vector.tensor_copy(out=affine[:], in_=as_columns[:, 0 : 2 * GATES * H_TILES])
 
         for step in range(-FLIP_AHEAD, N_TILES + LEAVE_BEHIND):
+            if step == 0:
+                spread_biases()
             if step == AFFINE_STEP:
                 prepare_affine()
             if is_tile(step + LOAD_AHEAD):

@@ -26,9 +26,9 @@ LOAD_AHEAD = 6
 FLIP_AHEAD = 3
 REGROUP_AHEAD = 2
 QUANT_AHEAD = 1
-MEAN_BEHIND = 1
-SQUARES_BEHIND = 2
-STD_BEHIND = 3
+PAIR = 2
+SQUARES_BEHIND = 1
+STATS_BEHIND = 2
 NORM_BEHIND = 4
 TURN_BEHIND = GROUP + NORM_BEHIND
 GATE_PRODUCT_BEHIND = TURN_BEHIND + 1
@@ -74,7 +74,7 @@ def tile_layernormlstmcell_pa_t_kernel(
         name="by_row", bufs=TURN_BEHIND + H_TILES
     ) as by_row, tc.tile_pool(name="by_feature", bufs=3) as by_feature, tc.tile_pool(
         name="gate_products", bufs=2 * H_TILES + 1
-    ) as gate_products, tc.tile_pool(name="stat", bufs=NORM_BEHIND + 2) as stat, tc.psum_pool(
+    ) as gate_products, tc.tile_pool(name="stat", bufs=4) as stat, tc.psum_pool(
         name="psum", bufs=2
     ) as psum:
         x_rows = {}
@@ -136,62 +136,65 @@ def tile_layernormlstmcell_pa_t_kernel(
                     stop=(operand == 1),
                 )
 
+        def column(r, gate):
+            first = GATES * (r % PAIR) + gate
+            return slice(first, first + 1)
+
         def add_bias(r, gate):
-            if gate == 0:
-                stats[r] = [stat.tile([P, GATES], F32, name="stat%d" % i) for i in range(5)]
+            if gate == 0 and r % PAIR == 0:
+                stats[r // PAIR] = [
+                    stat.tile([P, PAIR * GATES], F32, name="stat%d" % i) for i in range(5)
+                ]
             z[r, gate] = by_row.tile([P, H], F32, name="z%d" % gate)
             nc.vector.scalar_tensor_tensor(
                 out=z[r, gate][:],
                 in0=sums[r, gate][:],
-                scalar=1.0,
+                scalar=1.0 / H,
                 in1=bias_rows[gate][:],
                 op0=ALU.mult,
                 op1=ALU.add,
-                accum_out=stats[r][0][:, gate : gate + 1],
+                accum_out=stats[r // PAIR][0][:, column(r, gate)],
             )
 
-        def mean(r):
-            z_sum, neg_mean = stats[r][0], stats[r][1]
+        def squares(r, gate):
+            v_mean, sq_sum = stats[r // PAIR][0], stats[r // PAIR][2]
+            unused = by_feature.tile([P, H], BF16, name="unused%d" % gate)
+            nc.scalar.activation(
+                out=unused[:],
+                in_=z[r, gate][:],
+                func=ACT.Square,
+                bias=v_mean[:, column(r, gate)],
+                scale=-1.0 * H,
+                accum_out=sq_sum[:, column(r, gate)],
+            )
+
+        def pair_statistics(pair):
+            v_mean, neg_mean, sq_sum, var_eps, rstd = stats[pair]
+            nc.gpsimd.tensor_scalar(
+                out=var_eps[:],
+                in0=sq_sum[:],
+                scalar1=1.0 / (H * H * H),
+                scalar2=EPS / (H * H),
+                op0=ALU.mult,
+                op1=ALU.add,
+            )
+            nc.gpsimd.tensor_tensor(out=rstd[:], in0=var_eps[:], in1=neg_half[:], op=ALU.pow)
             nc.gpsimd.tensor_scalar(
                 out=neg_mean[:],
-                in0=z_sum[:],
+                in0=v_mean[:],
                 scalar1=-1.0 / H,
                 scalar2=0.0,
                 op0=ALU.mult,
                 op1=ALU.add,
             )
 
-        def squares(r, gate):
-            neg_mean, sq_sum = stats[r][1], stats[r][2]
-            unused = by_feature.tile([P, H], BF16, name="unused%d" % gate)
-            nc.scalar.activation(
-                out=unused[:],
-                in_=z[r, gate][:],
-                func=ACT.Square,
-                bias=neg_mean[:, gate : gate + 1],
-                scale=1.0,
-                accum_out=sq_sum[:, gate : gate + 1],
-            )
-
-        def inverse_std(r):
-            sq_sum, var_eps, rstd = stats[r][2], stats[r][3], stats[r][4]
-            nc.gpsimd.tensor_scalar(
-                out=var_eps[:],
-                in0=sq_sum[:],
-                scalar1=1.0 / H,
-                scalar2=EPS,
-                op0=ALU.mult,
-                op1=ALU.add,
-            )
-            nc.gpsimd.tensor_tensor(out=rstd[:], in0=var_eps[:], in1=neg_half[:], op=ALU.pow)
-
         def normalise(r, gate):
-            neg_mean, rstd = stats[r][1], stats[r][4]
+            neg_mean, rstd = stats[r // PAIR][1], stats[r // PAIR][4]
             nc.vector.tensor_scalar(
                 out=z[r, gate][:],
                 in0=z[r, gate][:],
-                scalar1=neg_mean[:, gate : gate + 1],
-                scalar2=rstd[:, gate : gate + 1],
+                scalar1=neg_mean[:, column(r, gate)],
+                scalar2=rstd[:, column(r, gate)],
                 op0=ALU.add,
                 op1=ALU.mult,
             )
@@ -264,7 +267,7 @@ def tile_layernormlstmcell_pa_t_kernel(
         nc.vector.memset(ones[:], 1.0)
         as_rows = const.tile([P, P], BF16)
         nc.vector.memset(as_rows[:], 0.0)
-        neg_half = const.tile([P, GATES], F32)
+        neg_half = const.tile([P, PAIR * GATES], F32)
         nc.vector.memset(neg_half[:], -0.5)
         ident = const.tile([P, P], F32)
         make_identity(nc, ident[:])
@@ -310,7 +313,14 @@ def tile_layernormlstmcell_pa_t_kernel(
                     stop=True,
                 )
                 bias_row = const.tile([P, H], F32, name="bias_row%d" % gate)
-                nc.vector.tensor_copy(out=bias_row[:], in_=repeated[:])
+                nc.vector.tensor_scalar(
+                    out=bias_row[:],
+                    in0=repeated[:],
+                    scalar1=1.0 / H,
+                    scalar2=0.0,
+                    op0=ALU.mult,
+                    op1=ALU.add,
+                )
                 bias_rows.append(bias_row)
 
         for v in range(2 * GATES):
@@ -338,10 +348,8 @@ def tile_layernormlstmcell_pa_t_kernel(
                 keep_clock()
             if is_tile(step - LEAVE_BEHIND):
                 leave(step - LEAVE_BEHIND)
-            if is_tile(step - STD_BEHIND):
-                inverse_std(step - STD_BEHIND)
-            if is_tile(step - MEAN_BEHIND):
-                mean(step - MEAN_BEHIND)
+            if is_tile(step - STATS_BEHIND) and (step - STATS_BEHIND) % PAIR == PAIR - 1:
+                pair_statistics((step - STATS_BEHIND) // PAIR)
             if is_tile(step):
                 add_bias(step, 0)
             if is_tile(step - TURN_BEHIND):

@@ -33,7 +33,7 @@ NORM_BEHIND = 4
 TURN_BEHIND = GROUP + NORM_BEHIND
 GATE_PRODUCT_BEHIND = TURN_BEHIND + 1
 AFFINE_STEP = TURN_BEHIND - 2
-BACK_BEHIND = GATE_PRODUCT_BEHIND + H_TILES
+BACK_BEHIND = GATE_PRODUCT_BEHIND + 1
 LEAVE_BEHIND = BACK_BEHIND + 1
 
 
@@ -73,7 +73,7 @@ def tile_layernormlstmcell_pa_t_kernel(
     ) as rows, tc.tile_pool(name="quant", bufs=3) as quant, tc.tile_pool(
         name="by_row", bufs=TURN_BEHIND + H_TILES
     ) as by_row, tc.tile_pool(name="by_feature", bufs=3) as by_feature, tc.tile_pool(
-        name="gate_products", bufs=2 * H_TILES + 1
+        name="gate_products", bufs=3
     ) as gate_products, tc.tile_pool(name="stat", bufs=4) as stat, tc.psum_pool(
         name="psum", bufs=2
     ) as psum:
@@ -229,21 +229,24 @@ def tile_layernormlstmcell_pa_t_kernel(
                 op=ALU.mult,
             )
 
-        def turn_back(r):
-            group, s = divmod(r, GROUP)
-            back[r] = psum.tile([P, H_TILES, P], F32, name="back")
-            for j in range(H_TILES):
-                nc.tensor.transpose(back[r][:, j, :], gated[group, j][:, s, :], ident[:])
+        def turn_back(group, j):
+            back[group, j] = psum.tile([P, GROUP, P], F32, name="back")
+            for s in range(GROUP):
+                nc.tensor.transpose(back[group, j][:, s, :], gated[group, j][:, s, :], ident[:])
 
-        def leave(r):
-            result = rows.tile([P, H], F32, name="result")
-            if r % 2 == 0 and (r + LEAVE_BEHIND < N_TILES or r >= N_TILES - GROUP):
-                nc.scalar.copy(out=result[:], in_=back[r][:].rearrange("p j f -> p (j f)"))
+        def leave(group, j):
+            r = group * H_TILES + j
+            result = rows.tile([P, GROUP, P], F32, name="result")
+            if r % 2 == 0 and r + LEAVE_BEHIND < N_TILES:
+                nc.scalar.copy(out=result[:], in_=back[group, j][:])
             else:
-                nc.vector.tensor_copy(
-                    out=result[:], in_=back[r][:].rearrange("p j f -> p (j f)")
-                )
-            nc.sync.dma_start(out=out[r * P : (r + 1) * P, :], in_=result[:])
+                nc.vector.tensor_copy(out=result[:], in_=back[group, j][:])
+            nc.sync.dma_start(
+                out=out[group * GROUP * P : (group + 1) * GROUP * P, j * P : (j + 1) * P].rearrange(
+                    "(s p) f -> p s f", p=P
+                ),
+                in_=result[:],
+            )
 
         def keep_clock():
             idle = psum.tile([P, H], F32, tag="sums")
@@ -344,10 +347,10 @@ def tile_layernormlstmcell_pa_t_kernel(
                 load(step + LOAD_AHEAD)
             if is_tile(step):
                 multiply(step, 0)
-            elif is_tile(step - TURN_BEHIND):
+            elif is_tile(step - BACK_BEHIND):
                 keep_clock()
             if is_tile(step - LEAVE_BEHIND):
-                leave(step - LEAVE_BEHIND)
+                leave(*divmod(step - LEAVE_BEHIND, H_TILES))
             if is_tile(step - STATS_BEHIND) and (step - STATS_BEHIND) % PAIR == PAIR - 1:
                 pair_statistics((step - STATS_BEHIND) // PAIR)
             if is_tile(step):
@@ -373,6 +376,6 @@ def tile_layernormlstmcell_pa_t_kernel(
                 normalise(step - NORM_BEHIND, 0)
                 normalise(step - NORM_BEHIND, 1)
             if is_tile(step - BACK_BEHIND):
-                turn_back(step - BACK_BEHIND)
+                turn_back(*divmod(step - BACK_BEHIND, H_TILES))
             if is_tile(step + FLIP_AHEAD):
                 flip(step + FLIP_AHEAD)

@@ -26,10 +26,10 @@ LOAD_AHEAD = 6
 FLIP_AHEAD = 3
 REGROUP_AHEAD = 2
 QUANT_AHEAD = 1
-PAIR = 2
+PAIR = 1
 SQUARES_BEHIND = 1
 STATS_BEHIND = 2
-NORM_BEHIND = 4
+NORM_BEHIND = 3
 TURN_BEHIND = GROUP + NORM_BEHIND
 GATE_PRODUCT_BEHIND = TURN_BEHIND + 1
 AFFINE_STEP = TURN_BEHIND - 2
@@ -237,7 +237,7 @@ def tile_layernormlstmcell_pa_t_kernel(
         def leave(group, j):
             r = group * H_TILES + j
             result = rows.tile([P, GROUP, P], F32, name="result")
-            if r % 2 == 0 and r + LEAVE_BEHIND < N_TILES:
+            if r % 5 in (0, 2) and r + LEAVE_BEHIND < N_TILES:
                 nc.scalar.copy(out=result[:], in_=back[group, j][:])
             else:
                 nc.vector.tensor_copy(out=result[:], in_=back[group, j][:])

@@ -272,6 +272,8 @@ def tile_layernormlstmcell_pa_t_kernel(
         nc.vector.memset(as_rows[:], 0.0)
         neg_half = const.tile([P, PAIR * GATES], F32)
         nc.vector.memset(neg_half[:], -0.5)
+        first_table = const.tile([P, PAIR * GATES], F32)
+        nc.scalar.activation(out=first_table[:], in_=neg_half[:], func=ACT.Sigmoid)
         ident = const.tile([P, P], F32)
         make_identity(nc, ident[:])
         ident_bf = const.tile([P, P], BF16)

@@ -171,6 +171,14 @@ def tile_layernormlstmcell_pa_t_kernel(
         def pair_statistics(pair):
             v_mean, neg_mean, sq_sum, var_eps, rstd = stats[pair]
             nc.gpsimd.tensor_scalar(
+                out=neg_mean[:],
+                in0=v_mean[:],
+                scalar1=-1.0 / H,
+                scalar2=0.0,
+                op0=ALU.mult,
+                op1=ALU.add,
+            )
+            nc.gpsimd.tensor_scalar(
                 out=var_eps[:],
                 in0=sq_sum[:],
                 scalar1=1.0 / (H * H * H),
@@ -179,14 +187,6 @@ def tile_layernormlstmcell_pa_t_kernel(
                 op1=ALU.add,
             )
             nc.gpsimd.tensor_tensor(out=rstd[:], in0=var_eps[:], in1=neg_half[:], op=ALU.pow)
-            nc.gpsimd.tensor_scalar(
-                out=neg_mean[:],
-                in0=v_mean[:],
-                scalar1=-1.0 / H,
-                scalar2=0.0,
-                op0=ALU.mult,
-                op1=ALU.add,
-            )
 
         def normalise(r, gate):
             neg_mean, rstd = stats[r // PAIR][1], stats[r // PAIR][4]

@@ -178,14 +178,15 @@ def tile_layernormlstmcell_pa_t_kernel(
                 op0=ALU.mult,
                 op1=ALU.add,
             )
-            nc.gpsimd.tensor_scalar(
-                out=var_eps[:],
-                in0=sq_sum[:],
-                scalar1=1.0 / (H * H * H),
-                scalar2=EPS / (H * H),
-                op0=ALU.mult,
-                op1=ALU.add,
-            )
+            if pair < N_TILES - 1:
+                nc.gpsimd.tensor_scalar(
+                    out=var_eps[:],
+                    in0=sq_sum[:],
+                    scalar1=1.0 / (H * H * H),
+                    scalar2=EPS / (H * H),
+                    op0=ALU.mult,
+                    op1=ALU.add,
+                )
             nc.gpsimd.tensor_tensor(out=rstd[:], in0=var_eps[:], in1=neg_half[:], op=ALU.pow)
 
         def normalise(r, gate):
@@ -366,6 +367,9 @@ def tile_layernormlstmcell_pa_t_kernel(
                 regroup(step + REGROUP_AHEAD)
             if is_tile(step + QUANT_AHEAD):
                 quantise(step + QUANT_AHEAD)
+            if step - NORM_BEHIND == N_TILES - 1:
+                normalise(step - NORM_BEHIND, 0)
+                normalise(step - NORM_BEHIND, 1)
             if is_tile(step - GATE_PRODUCT_BEHIND):
                 gate_product(*divmod(step - GATE_PRODUCT_BEHIND, H_TILES))
             if is_tile(step):
@@ -374,7 +378,15 @@ def tile_layernormlstmcell_pa_t_kernel(
             if is_tile(step - SQUARES_BEHIND):
                 squares(step - SQUARES_BEHIND, 0)
                 squares(step - SQUARES_BEHIND, 1)
-            if is_tile(step - NORM_BEHIND):
+            if step - SQUARES_BEHIND == N_TILES - 1:
+                nc.scalar.activation(
+                    out=stats[N_TILES - 1][3][:],
+                    in_=stats[N_TILES - 1][2][:],
+                    func=ACT.Copy,
+                    bias=EPS / (H * H),
+                    scale=1.0 / (H * H * H),
+                )
+            if is_tile(step - NORM_BEHIND) and step - NORM_BEHIND < N_TILES - 1:
                 normalise(step - NORM_BEHIND, 0)
                 normalise(step - NORM_BEHIND, 1)
             if is_tile(step - BACK_BEHIND):

import concourse.mybir as mybir
from concourse.masks import make_identity

F32 = mybir.dt.float32
BF16 = mybir.dt.bfloat16
U8 = mybir.dt.uint8
U32 = mybir.dt.uint32
I32 = mybir.dt.int32
FP8X4 = mybir.dt.float8_e4m3fn_x4
ALU = mybir.AluOpType
ACT = mybir.ActivationFunctionType

P = 128
B = 4096
K = 512
H = 512
H_TILES = H // P
EPS = 1e-5
N_TILES = B // P
GROUP = 4
GATES = 2
FLOPS = 2 * B * (2 * K) * (GATES * H)

FIRST_TILES = 3
LOAD_AHEAD = 6
FLIP_AHEAD = 3
REGROUP_AHEAD = 2
QUANT_AHEAD = 1
PAIR = 1
SQUARES_BEHIND = 1
STATS_BEHIND = 2
NORM_BEHIND = 3
TURN_BEHIND = GROUP + NORM_BEHIND
GATE_PRODUCT_BEHIND = TURN_BEHIND + 1
AFFINE_STEP = TURN_BEHIND - 2
BACK_BEHIND = GATE_PRODUCT_BEHIND + 1
LEAVE_BEHIND = BACK_BEHIND + 1


def tile_layernormlstmcell_pa_t_kernel(
    tc,
    x,
    h,
    Wi_w_words,
    Wi_w_scales,
    Wi_b,
    Ui_w_words,
    Ui_w_scales,
    lni_g,
    lni_b,
    Wc_w_words,
    Wc_w_scales,
    Wc_b,
    Uc_w_words,
    Uc_w_scales,
    lnc_g,
    lnc_b,
    out,
):
    nc = tc.nc
    weights = [
        (Wi_w_words, Wi_w_scales),
        (Ui_w_words, Ui_w_scales),
        (Wc_w_words, Wc_w_scales),
        (Uc_w_words, Uc_w_scales),
    ]
    biases = [Wi_b, Wc_b]
    gains_shifts = [lni_g, lni_b, lnc_g, lnc_b]
    functions = [ACT.Sigmoid, ACT.Tanh]

    with tc.manual_schedule(), tc.tile_pool(name="const", bufs=1) as const, tc.tile_pool(
        name="rows", bufs=LOAD_AHEAD - FLIP_AHEAD + 2
    ) as rows, tc.tile_pool(name="quant", bufs=3) as quant, tc.tile_pool(
        name="by_row", bufs=TURN_BEHIND + H_TILES
    ) as by_row, tc.tile_pool(name="by_feature", bufs=3) as by_feature, tc.tile_pool(
        name="gate_products", bufs=3
    ) as gate_products, tc.tile_pool(name="stat", bufs=4) as stat, tc.psum_pool(
        name="psum", bufs=2
    ) as psum:
        x_rows = {}
        h_rows = {}
        flipped = {}
        grouped = {}
        codes = {}
        scales = {}
        sums = {}
        z = {}
        stats = {}
        turned = {}
        acted = {}
        gated = {}
        back = {}

        def load(r):
            tile_rows = slice(r * P, (r + 1) * P)
            x_rows[r] = rows.tile([P, K], BF16, name="x_rows")
            nc.sync.dma_start(out=x_rows[r][:], in_=x[tile_rows, :])
            h_rows[r] = rows.tile([P, K], BF16, name="h_rows")
            nc.sync.dma_start(out=h_rows[r][:], in_=h[tile_rows, :])

        def flip(r):
            flipped[r] = psum.tile([P, 4, P], F32, name="flipped")
            for operand, src in enumerate((x_rows[r], h_rows[r])):
                pairs = src[:].bitcast(F32)
                for u in range(2):
                    nc.tensor.transpose(
                        flipped[r][:, 2 * operand + u, :], pairs[:, u : K // 2 : 2], ident[:]
                    )

        def regroup(r):
            grouped[r] = quant.tile([P, 2 * P * 4], BF16, name="grouped", align_bytes=64)
            nc.scalar.copy(
                out=grouped[r][:].bitcast(F32).rearrange("p (o r u) -> p o r u", o=2, u=2),
                in_=flipped[r][:].rearrange("p (o u) r -> p o r u", u=2),
            )

        def quantise(r):
            codes[r] = quant.tile([P, 2 * P], U32, name="codes", align_bytes=64)
            scales[r] = quant.tile([P, 2 * P], U8, name="scales", align_bytes=64)
            nc.vector.quantize_mx(
                out=codes[r][:].bitcast(FP8X4), scales=scales[r][:], in_=grouped[r][:]
            )

        def multiply(r, gate):
            sums[r, gate] = psum.tile([P, H], F32, name="sums")
            for operand in range(2):
                w = 2 * gate + operand
                cols = slice(operand * P, (operand + 1) * P)
                nc.tensor.matmul_mx(
                    out=sums[r, gate][:],
                    lhsT=codes[r][:, cols].bitcast(FP8X4),
                    lhsT_scale=scales[r][:, cols],
                    rhs=w_words[w][:].bitcast(FP8X4),
                    rhs_scale=planes[4 * w : P, :],
                    start=(operand == 0),
                    stop=(operand == 1),
                )

        def column(r, gate):
            first = GATES * (r % PAIR) + gate
            return slice(first, first + 1)

        def add_bias(r, gate):
            if gate == 0 and r % PAIR == 0:
                stats[r // PAIR] = [
                    stat.tile([P, PAIR * GATES], F32, name="stat%d" % i) for i in range(5)
                ]
            z[r, gate] = by_row.tile([P, H], F32, name="z%d" % gate)
            nc.vector.scalar_tensor_tensor(
                out=z[r, gate][:],
                in0=sums[r, gate][:],
                scalar=1.0 / H,
                in1=bias_rows[gate][:],
                op0=ALU.mult,
                op1=ALU.add,
                accum_out=stats[r // PAIR][0][:, column(r, gate)],
            )

        def squares(r, gate):
            v_mean, sq_sum = stats[r // PAIR][0], stats[r // PAIR][2]
            unused = by_feature.tile([P, H], BF16, name="unused%d" % gate)
            nc.scalar.activation(
                out=unused[:],
                in_=z[r, gate][:],
                func=ACT.Square,
                bias=v_mean[:, column(r, gate)],
                scale=-1.0 * H,
                accum_out=sq_sum[:, column(r, gate)],
            )

        def pair_statistics(pair):
            v_mean, neg_mean, sq_sum, var_eps, rstd = stats[pair]
            nc.gpsimd.tensor_scalar(
                out=neg_mean[:],
                in0=v_mean[:],
                scalar1=-1.0 / H,
                scalar2=0.0,
                op0=ALU.mult,
                op1=ALU.add,
            )
            if pair < N_TILES - 1:
                nc.gpsimd.tensor_scalar(
                    out=var_eps[:],
                    in0=sq_sum[:],
                    scalar1=1.0 / (H * H * H),
                    scalar2=EPS / (H * H),
                    op0=ALU.mult,
                    op1=ALU.add,
                )
            nc.gpsimd.tensor_tensor(out=rstd[:], in0=var_eps[:], in1=neg_half[:], op=ALU.pow)

        def normalise(r, gate):
            neg_mean, rstd = stats[r // PAIR][1], stats[r // PAIR][4]
            nc.vector.tensor_scalar(
                out=z[r, gate][:],
                in0=z[r, gate][:],
                scalar1=neg_mean[:, column(r, gate)],
                scalar2=rstd[:, column(r, gate)],
                op0=ALU.add,
                op1=ALU.mult,
            )

        def turn(group, j, gate):
            turned[group, j, gate] = psum.tile([P, GROUP, P], F32, name="turned")
            for s in range(GROUP):
                nc.tensor.transpose(
                    turned[group, j, gate][:, s, :],
                    z[group * GROUP + s, gate][:, j * P : (j + 1) * P],
                    ident[:],
                )

        def activate(group, j, gate):
            acted[group, j, gate] = by_feature.tile([P, GROUP, P], F32, name="acted%d" % gate)
            gain = (2 * gate) * H_TILES + j
            shift = (2 * gate + 1) * H_TILES + j
            nc.scalar.activation(
                out=acted[group, j, gate][:],
                in_=turned[group, j, gate][:],
                func=functions[gate],
                bias=affine[:, shift : shift + 1],
                scale=affine[:, gain : gain + 1],
            )

        def gate_product(group, j):
            gated[group, j] = gate_products.tile([P, GROUP, P], F32, name="gated")
            nc.vector.tensor_tensor(
                out=gated[group, j][:],
                in0=acted[group, j, 0][:],
                in1=acted[group, j, 1][:],
                op=ALU.mult,
            )

        def turn_back(group, j):
            back[group, j] = psum.tile([P, GROUP, P], F32, name="back")
            for s in range(GROUP):
                nc.tensor.transpose(back[group, j][:, s, :], gated[group, j][:, s, :], ident[:])

        def leave(group, j):
            r = group * H_TILES + j
            result = rows.tile([P, GROUP, P], F32, name="result")
            if r % 5 in (0, 2) and r + LEAVE_BEHIND < N_TILES:
                nc.scalar.copy(out=result[:], in_=back[group, j][:])
            else:
                nc.vector.tensor_copy(out=result[:], in_=back[group, j][:])
            nc.sync.dma_start(
                out=out[group * GROUP * P : (group + 1) * GROUP * P, j * P : (j + 1) * P].rearrange(
                    "(s p) f -> p s f", p=P
                ),
                in_=result[:],
            )

        def keep_clock():
            idle = psum.tile([P, H], F32, tag="sums")
            for gate in range(GATES):
                nc.tensor.matmul(
                    out=idle[:], lhsT=ones[:], rhs=bias_in_row_0[:, gate, :], start=True, stop=True
                )

        def is_tile(r):
            return 0 <= r < N_TILES

        planes = const.tile([P, H], U8, align_bytes=64)
        nc.vector.memset(planes[:].bitcast(I32), 0)
        bias_in_row_0 = const.tile([P, GATES, H], BF16)
        nc.vector.memset(bias_in_row_0[:], 0.0)
        for gate in range(GATES):
            nc.gpsimd.dma_start(
                out=bias_in_row_0[0:1, gate, :], in_=biases[gate].rearrange("(o n) -> o n", o=1)
            )
        ones = const.tile([P, P], BF16)
        nc.vector.memset(ones[:], 1.0)
        as_rows = const.tile([P, P], BF16)
        nc.vector.memset(as_rows[:], 0.0)
        neg_half = const.tile([P, PAIR * GATES], F32)
        nc.vector.memset(neg_half[:], -0.5)
        first_table = const.tile([P, PAIR * GATES], F32)
        nc.scalar.activation(out=first_table[:], in_=neg_half[:], func=ACT.Sigmoid)
        ident = const.tile([P, P], F32)
        make_identity(nc, ident[:])
        ident_bf = const.tile([P, P], BF16)
        make_identity(nc, ident_bf[:])

        first_x = const.tile([P, FIRST_TILES, K], BF16)
        first_h = const.tile([P, FIRST_TILES, K], BF16)
        for first, operand in ((first_x, x), (first_h, h)):
            nc.sync.dma_start(
                out=first[:], in_=operand[0 : FIRST_TILES * P, :].rearrange("(s p) k -> p s k", p=P)
            )
        for r in range(FIRST_TILES):
            x_rows[r] = first_x[:, r, :]
            h_rows[r] = first_h[:, r, :]
        w_words = []
        for w in range(2 * GATES):
            for quad in range(4):
                first = 32 * quad + 4 * w
                nc.sync.dma_start(
                    out=planes[first : first + 4, :].bitcast(I32),
                    in_=weights[w][1][0, 4 * quad : 4 * quad + 4, :].bitcast(I32),
                )
            if w % 2 == 1:
                for loaded in (w - 1, w):
                    words = const.tile([P, H], U32, name="words%d" % loaded, align_bytes=64)
                    nc.sync.dma_start(
                        out=words[:].bitcast(I32),
                        in_=weights[loaded][0][0].rearrange("p n t -> p (n t)").bitcast(I32),
                    )
                    w_words.append(words)

        bias_rows = []

        def spread_biases():
            for gate in range(GATES):
                repeated = psum.tile([P, H], F32, tag="sums")
                nc.tensor.matmul(
                    out=repeated[:],
                    lhsT=ones[:],
                    rhs=bias_in_row_0[:, gate, :],
                    start=True,
                    stop=True,
                )
                bias_row = const.tile([P, H], F32, name="bias_row%d" % gate)
                nc.vector.tensor_scalar(
                    out=bias_row[:],
                    in0=repeated[:],
                    scalar1=1.0 / H,
                    scalar2=0.0,
                    op0=ALU.mult,
                    op1=ALU.add,
                )
                bias_rows.append(bias_row)

        for v in range(2 * GATES):
            nc.gpsimd.dma_start(
                out=as_rows[H_TILES * v : H_TILES * (v + 1), :],
                in_=gains_shifts[v].rearrange("(j f) -> j f", f=P),
            )
        affine = const.tile([P, 2 * GATES * H_TILES], F32)

        def prepare_affine():
            as_columns = psum.tile([P, P], BF16, tag="back")
            nc.tensor.transpose(as_columns[:], as_rows[:], ident_bf[:])
            nc.vector.tensor_copy(out=affine[:], in_=as_columns[:, 0 : 2 * GATES * H_TILES])

        for step in range(-FLIP_AHEAD, N_TILES + LEAVE_BEHIND):
            if step == 0:
                spread_biases()
            if step == AFFINE_STEP:
                prepare_affine()
            if is_tile(step + LOAD_AHEAD):
                load(step + LOAD_AHEAD)
            if is_tile(step):
                multiply(step, 0)
            elif is_tile(step - BACK_BEHIND):
                keep_clock()
            if is_tile(step - LEAVE_BEHIND):
                leave(*divmod(step - LEAVE_BEHIND, H_TILES))
            if is_tile(step - STATS_BEHIND) and (step - STATS_BEHIND) % PAIR == PAIR - 1:
                pair_statistics((step - STATS_BEHIND) // PAIR)
            if is_tile(step):
                add_bias(step, 0)
            if is_tile(step - TURN_BEHIND):
                group, j = divmod(step - TURN_BEHIND, H_TILES)
                for gate in range(GATES):
                    turn(group, j, gate)
                    activate(group, j, gate)
            if is_tile(step + REGROUP_AHEAD):
                regroup(step + REGROUP_AHEAD)
            if is_tile(step + QUANT_AHEAD):
                quantise(step + QUANT_AHEAD)
            if step - NORM_BEHIND == N_TILES - 1:
                normalise(step - NORM_BEHIND, 0)
                normalise(step - NORM_BEHIND, 1)
            if is_tile(step - GATE_PRODUCT_BEHIND):
                gate_product(*divmod(step - GATE_PRODUCT_BEHIND, H_TILES))
            if is_tile(step):
                multiply(step, 1)
                add_bias(step, 1)
            if is_tile(step - SQUARES_BEHIND):
                squares(step - SQUARES_BEHIND, 0)
                squares(step - SQUARES_BEHIND, 1)
            if step - SQUARES_BEHIND == N_TILES - 1:
                nc.scalar.activation(
                    out=stats[N_TILES - 1][3][:],
                    in_=stats[N_TILES - 1][2][:],
                    func=ACT.Copy,
                    bias=EPS / (H * H),
                    scale=1.0 / (H * H * H),
                )
            if is_tile(step - NORM_BEHIND) and step - NORM_BEHIND < N_TILES - 1:
                normalise(step - NORM_BEHIND, 0)
                normalise(step - NORM_BEHIND, 1)
            if is_tile(step - BACK_BEHIND):
                turn_back(*divmod(step - BACK_BEHIND, H_TILES))
            if is_tile(step + FLIP_AHEAD):
                flip(step + FLIP_AHEAD)
